import numpy as np
import ml_dtypes


def mxq(x, axis, fmt="e4m3"):
    dtype, down = {"e4m3": (ml_dtypes.float8_e4m3fn, 7), "e5m2": (ml_dtypes.float8_e5m2, 14)}[fmt]
    v = np.moveaxis(np.asarray(x, np.float32).astype(ml_dtypes.bfloat16).astype(np.float64), axis, -1)
    blocks = v.reshape(v.shape[:-1] + (-1, 32))
    amax = np.abs(blocks).max(-1, keepdims=True)
    byte = np.maximum(np.where(amax > 0, np.frexp(amax)[1] - 1 + 127, 0) - down, 1)
    scale = np.exp2(byte - 127.0)
    codes = (blocks / scale).astype(np.float32).astype(dtype).astype(np.float64)
    return np.moveaxis((codes * scale).reshape(v.shape), -1, axis)


WIDE = False


def mx_kscale(k):
    if not WIDE:
        return np.ones(k)
    levels = np.array([10, -10, 5, -5, 0])
    if k % 512:
        return np.exp2(np.random.permutation(np.resize(levels, k // 32))).repeat(32)
    a = np.empty((k // 512, 16))
    for p in range(k // 512):
        a[p, :8] = np.random.permutation(np.resize(levels, 8))
        for g in range(8):
            far = levels[np.abs(levels - a[p, g]) >= 10]
            a[p, g + 8] = far[np.random.randint(len(far))]
    return np.exp2(a.ravel()).repeat(32)


BF16 = ml_dtypes.bfloat16


def bf(x):
    return np.asarray(x, np.float32).astype(BF16)


def f64(x):
    return np.asarray(x).astype(np.float64)


E2M1 = np.array([0.0, 0.5, 1.0, 1.5, 2.0, 3.0, 4.0, 6.0, -0.0, -0.5, -1.0, -1.5, -2.0, -3.0, -4.0, -6.0])


def pack_weight(w, fmt):
    k, n = w.shape
    w = f64(bf(w)).reshape(k // 32, 32, n)
    amax = np.abs(w).max(1)
    if fmt == "e4m3":
        byte = np.frexp(amax)[1] - 1 + 127 - 7
    else:
        mant, ex = np.frexp(amax / 6.0)
        byte = np.where(mant > 0.5, ex, ex - 1) + 127
    byte = np.clip(np.where(amax > 0, byte, 1), 1, 254)
    scaled = (w * np.exp2(127.0 - byte)[:, None, :]).reshape(k, n).astype(np.float32)
    by_word = np.ascontiguousarray(scaled.reshape(k // 512, 128, 4, n).transpose(0, 1, 3, 2))
    if fmt == "e4m3":
        words = by_word.astype(ml_dtypes.float8_e4m3fn).view(np.uint8)
    else:
        c = by_word.astype(ml_dtypes.float4_e2m1fn).view(np.uint8) & 0xF
        words = c[..., 0::2] | (c[..., 1::2] << 4)
    return np.ascontiguousarray(words), np.ascontiguousarray(byte.astype(np.uint8).reshape(k // 512, 16, n))


def unpack_weight(words, scales, fmt):
    g, p, n, _ = words.shape
    if fmt == "e4m3":
        vals = np.ascontiguousarray(words).view(ml_dtypes.float8_e4m3fn).astype(np.float64)
    else:
        nib = np.empty((g, p, n, 4), np.uint8)
        nib[..., 0::2] = words & 0xF
        nib[..., 1::2] = words >> 4
        vals = E2M1[nib]
    vals = vals * np.repeat(np.exp2(scales.astype(np.float64) - 127.0), 8, axis=1)[..., None]
    return vals.transpose(0, 1, 3, 2).reshape(g * 512, n)
def pack4(w):
    words, scales = pack_weight(w, "e2m1")
    return words.reshape(words.shape[0], 128, -1), scales


def unpack4(words, scales):
    return unpack_weight(words.reshape(words.shape[0], 128, -1, 2), scales, "e2m1")


B, S, H, F = 512, 8, 512, 512


def draw0():
    s = mx_kscale(H)
    t = mx_kscale(F)
    s2 = np.concatenate([s, s])
    h = bf(np.random.standard_normal((B, S, H)) * s)
    ew1_words, ew1_scales = pack4(np.random.standard_normal((2 * H, F)) / np.sqrt(2 * H) / s2[:, None] * t)
    eb1 = bf(np.random.standard_normal(F) * 0.3 * t)
    ew2_words, ew2_scales = pack4(np.random.standard_normal((F, H)) / np.sqrt(F) / t[:, None])
    eb2 = bf(np.random.standard_normal(H) * 0.3)
    return {"h": h,
            "ew1_words": ew1_words,
            "ew1_scales": ew1_scales,
            "eb1": eb1,
            "ew2_words": ew2_words,
            "ew2_scales": ew2_scales,
            "eb2": eb2}


def edge_mlp(xq, w1q, b1, w2q, b2):
    hid = np.maximum((xq @ w1q) + b1, 0.0)
    return (mxq(hid, 2, "e4m3") @ w2q) + b2


def core(h, ew1_words, ew1_scales, eb1, ew2_words, ew2_scales, eb2):
    hq = mxq(f64(h), 2, "e4m3")
    w1q = unpack4(ew1_words, ew1_scales)
    w2q = unpack4(ew2_words, ew2_scales)
    b1, b2 = f64(eb1), f64(eb2)
    left = hq[:, :-1, :]
    right = hq[:, 1:, :]
    m_lr = edge_mlp(np.concatenate([left, right], axis=-1), w1q, b1, w2q, b2)
    m_rl = edge_mlp(np.concatenate([right, left], axis=-1), w1q, b1, w2q, b2)
    zcol = np.zeros_like(m_lr[:, :1, :])
    return np.concatenate([zcol, m_lr], axis=1) + np.concatenate([m_rl, zcol], axis=1)


def e4m3fn_bytes(y):
    return np.clip(np.asarray(y, np.float64), -448.0, 448.0).astype(np.float32).astype(ml_dtypes.float8_e4m3fn).view(np.uint8)


def e4m3fn_values(b):
    return np.asarray(b, np.uint8).view(ml_dtypes.float8_e4m3fn).astype(np.float64)


def setup_inputs():
    d = draw0()
    x0 = np.asarray(d['h']).astype(np.float64)
    s = (np.max(np.abs(x0), axis=(0, 1), keepdims=True) / 448.0).astype(np.float32)
    out = {}
    for k, v in d.items():
        if k == 'h':
            out['h_bytes'] = e4m3fn_bytes(x0 / s.astype(np.float64))
            out['h_scale'] = s
        else:
            out[k] = v
    return out


def reference(h_bytes, h_scale, ew1_words, ew1_scales, eb1, ew2_words, ew2_scales, eb2):
    return core(e4m3fn_values(h_bytes) * h_scale.astype(np.float64), ew1_words, ew1_scales, eb1, ew2_words, ew2_scales, eb2)

@@ -1,0 +1,274 @@
+from contextlib import ExitStack
+
+import concourse.mybir as mybir
+from concourse.masks import make_identity
+
+F32 = mybir.dt.float32
+BF16 = mybir.dt.bfloat16
+I32 = mybir.dt.int32
+U32 = mybir.dt.uint32
+U8 = mybir.dt.uint8
+FP8 = mybir.dt.float8_e4m3fn
+E4M3X4 = mybir.dt.float8_e4m3fn_x4
+E2M1X4 = mybir.dt.float4_e2m1fn_x4
+ALU = mybir.AluOpType
+ACT = mybir.ActivationFunctionType
+
+P = 128
+B, S, H, F = 512, 8, 512, 512
+NC = B // P
+NT = F // P
+HALF = B // 2
+FLOPS = 2 * 2 * B * (S - 1) * (2 * H * F + F * H)
+
+RL, LR = "rl", "lr"
+
+
+def tile_graphnetlayer_pa_t_w4_kernel(tc, h_bytes, h_scale, ew1_words, ew1_scales, eb1, ew2_words, ew2_scales, eb2, out):
+    nc = tc.nc
+    with ExitStack() as ctx:
+        keep = ctx.enter_context(tc.tile_pool(name="keep", bufs=1))
+        work = ctx.enter_context(tc.tile_pool(name="work", bufs=2))
+        psum = ctx.enter_context(tc.psum_pool(name="psum", bufs=1))
+
+        hb = keep.tile([P, NC, S, H], U8, name="hb", align_bytes=64)
+        sc = keep.tile([P, H], F32, name="sc", align_bytes=64)
+        w1_raw = keep.tile([P, 2, 2 * F], U8, name="w1_raw", align_bytes=64)
+        w1 = keep.tile([P, 2, 2 * F], U8, name="w1", align_bytes=64)
+        w1s_raw = keep.tile([P, 2, F], U8, name="w1s_raw", align_bytes=64)
+        w1s = keep.tile([P, 2, F], U8, name="w1s", align_bytes=64)
+        w2 = keep.tile([P, 2 * H], U8, name="w2", align_bytes=64)
+        w2s = keep.tile([P, H], U8, name="w2s", align_bytes=64)
+        b1 = keep.tile([P, NT], BF16, name="b1", align_bytes=64)
+        b2_once = keep.tile([P, H], BF16, name="b2_once", align_bytes=64)
+        b2_twice = keep.tile([P, H], BF16, name="b2_twice", align_bytes=64)
+        ident = keep.tile([P, P], F32, name="ident", align_bytes=64)
+        dummy = keep.tile([P, 1], F32, name="dummy", align_bytes=64)
+
+
+        src = h_bytes.rearrange("(c p) s h -> p c s h", p=P)
+        nc.scalar.dma_start(out=sc[:], in_=h_scale.rearrange("a b k -> (a b k)").partition_broadcast(P))
+        nc.sync.dma_start(out=w1_raw[:], in_=ew1_words.rearrange("g p n -> p g n"))
+        nc.sync.dma_start(out=hb[:, 0:2, 0:2, :], in_=src[:, 0:2, 0:2, :])
+        nc.sync.dma_start(out=hb[:, 2:4, 0:2, :], in_=src[:, 2:4, 0:2, :])
+        nc.vector.memset(w1s_raw[:].rearrange("p g n -> p (g n)").bitcast(I32), 0)
+        nc.vector.memset(w2s[:].bitcast(I32), 0)
+        nc.vector.memset(dummy[:], 0.0)
+        for q in range(4):
+            nc.sync.dma_start(out=w1s_raw[32 * q : 32 * q + 4, :, :].bitcast(I32), in_=ew1_scales.bitcast(I32)[:, 4 * q : 4 * q + 4, :].rearrange("g q n -> q g n"))
+        nc.scalar.dma_start(out=b1[:], in_=eb1.rearrange("(p t) -> p t", t=NT))
+        make_identity(nc, ident[:])
+        nc.scalar.activation(out=dummy[:], in_=dummy[:], func=ACT.Relu)
+        nc.sync.dma_start(out=hb[:, :, 2:5, :], in_=src[:, :, 2:5, :])
+        nc.sync.dma_start(out=w2[:], in_=ew2_words[0])
+        for q in range(4):
+            nc.sync.dma_start(out=w2s[32 * q : 32 * q + 4, :].bitcast(I32), in_=ew2_scales[0].bitcast(I32)[4 * q : 4 * q + 4, :])
+        nc.sync.dma_start(out=hb[:, :, 5:8, :], in_=src[:, :, 5:8, :])
+        nc.sync.dma_start(out=b2_once[:], in_=eb2.partition_broadcast(P))
+
+        x = {}
+        xt = {}
+        hq = {}
+        pairs = {}
+        grouped = {}
+        hid = {}
+        acc1 = {}
+        acc2 = {}
+
+        def widen(j, c):
+            if j not in x:
+                x[j] = work.tile([P, NC, H], BF16, name="x", bufs=3, align_bytes=64)
+            nc.vector.tensor_tensor(out=x[j][:, c, :], in0=hb[:, c, j, :].bitcast(FP8), in1=sc[:], op=ALU.mult)
+
+        def turn(j, half):
+            bank = psum.tile([P, 2, 2, P], F32, name="xt", bufs=2)
+            xt[j, half] = bank
+            for cc in range(2):
+                words = x[j][:, 2 * half + cc, :].bitcast(F32)
+                for u in range(2):
+                    nc.tensor.transpose(bank[:, cc, u, :], words[:, u : 2 * P : 2], ident[:])
+
+        def words_out(j, half):
+            if j not in grouped:
+                grouped[j] = work.tile([P, NC, P, 4], BF16, name="grouped", bufs=2, align_bytes=64)
+            dst = grouped[j][:, 2 * half : 2 * half + 2, :, :].rearrange("p c r t -> p (c r t)").bitcast(F32)
+            nc.scalar.copy(out=dst.rearrange("p (c r u) -> p c r u", c=2, u=2), in_=xt[j, half][:].rearrange("p c u r -> p c r u"))
+
+        def quant_h(j):
+            codes = keep.tile([P, B], U32, name="hq%d" % j, align_bytes=64)
+            scales = keep.tile([P, B], U8, name="hs%d" % j, align_bytes=64)
+            hq[j] = (codes, scales)
+            nc.vector.quantize_mx(out=codes[:].bitcast(E4M3X4), scales=scales[:], in_=grouped[j][:].rearrange("p c r t -> p (c r t)"))
+
+        def first(i, d, t):
+            bank = psum.tile([P, B], F32, name="acc1", bufs=4)
+            acc1[i, d, t] = bank
+            nodes = (i, i + 1) if d == LR else (i + 1, i)
+            for g in range(2):
+                codes, scales = hq[nodes[g]]
+                nc.tensor.matmul_mx(
+                    out=bank[:],
+                    lhsT=w1[:, g, 256 * t : 256 * (t + 1)].bitcast(E2M1X4),
+                    lhsT_scale=w1s[:, g, P * t : P * (t + 1)],
+                    rhs=codes[:].bitcast(E4M3X4),
+                    rhs_scale=scales[:],
+                    start=(g == 0),
+                    stop=(g == 1),
+                )
+
+        def relu(i, d, t):
+            if (i, d) not in pairs:
+                pairs[i, d] = work.tile([P, 2, B, 2], BF16, name="pairs", bufs=3, align_bytes=64)
+            nc.scalar.activation(out=pairs[i, d][:, t // 2, :, t % 2], in_=acc1[i, d, t][:], func=ACT.Relu, bias=b1[:, t : t + 1])
+
+        def quant_h_half(j, half):
+            if j not in hq:
+                codes = keep.tile([P, B], U32, name="hq%d" % j, align_bytes=64)
+                scales = keep.tile([P, B], U8, name="hs%d" % j, align_bytes=64)
+                hq[j] = (codes, scales)
+            codes, scales = hq[j]
+            cols = slice(HALF * half, HALF * (half + 1))
+            nc.vector.quantize_mx(out=codes[:, cols].bitcast(E4M3X4), scales=scales[:, cols], in_=grouped[j][:, 2 * half : 2 * half + 2, :, :].rearrange("p c r t -> p (c r t)"))
+
+        def first_half(i, d, u, half):
+            bank = psum.tile([P, 2, HALF], F32, name="acc1", bufs=4)
+            nodes = (i, i + 1) if d == LR else (i + 1, i)
+            for e in range(2):
+                t = 2 * u + e
+                for c in range(2):
+                    cols = slice(HALF * half + P * c, HALF * half + P * (c + 1))
+                    for g in range(2):
+                        codes, scales = hq[nodes[g]]
+                        nc.tensor.matmul_mx(
+                            out=bank[:, e, P * c : P * (c + 1)],
+                            lhsT=w1[:, g, 256 * t : 256 * (t + 1)].bitcast(E2M1X4),
+                            lhsT_scale=w1s[:, g, P * t : P * (t + 1)],
+                            rhs=codes[:, cols].bitcast(E4M3X4),
+                            rhs_scale=scales[:, cols],
+                            start=(g == 0),
+                            stop=(g == 1),
+                        )
+            if (i, d) not in pairs:
+                pairs[i, d] = work.tile([P, 2, B, 2], BF16, name="pairs", bufs=3, align_bytes=64)
+            for e in range(2):
+                t = 2 * u + e
+                nc.scalar.activation(out=pairs[i, d][:, u, HALF * half : HALF * (half + 1), e], in_=bank[:, e, :], func=ACT.Relu, bias=b1[:, t : t + 1])
+
+        def inter_half(i, d, half):
+            if (i, d) not in grouped:
+                full = work.tile([P, 4 * B], BF16, name="full", bufs=2, align_bytes=64)
+                grouped[i, d] = full
+            full = grouped[i, d]
+            words = pairs[i, d][:].rearrange("p u n e -> p (u n e)").bitcast(F32).rearrange("p (u n) -> p n u", u=2)
+            cols = slice(HALF * half, HALF * (half + 1))
+            nc.vector.tensor_copy(out=full[:].bitcast(F32).rearrange("p (n u) -> p n u", u=2)[:, cols, :], in_=words[:, cols, :])
+
+        def quant_half(i, d, half):
+            if (i, d) not in hid:
+                codes = work.tile([P, B], U32, name="hidq", bufs=6, align_bytes=64)
+                scales = work.tile([P, B], U8, name="hids", bufs=6, align_bytes=64)
+                hid[i, d] = (codes, scales)
+            codes, scales = hid[i, d]
+            cols = slice(HALF * half, HALF * (half + 1))
+            nc.vector.quantize_mx(out=codes[:, cols].bitcast(E4M3X4), scales=scales[:, cols], in_=grouped[i, d][:, 4 * HALF * half : 4 * HALF * (half + 1)])
+
+        def inter(i, d):
+            full = work.tile([P, 4 * B], BF16, name="full", bufs=2, align_bytes=64)
+            grouped[i, d] = full
+            words = pairs[i, d][:].rearrange("p u n e -> p (u n e)").bitcast(F32)
+            nc.vector.tensor_copy(out=full[:].bitcast(F32).rearrange("p (n u) -> p n u", u=2), in_=words.rearrange("p (u n) -> p n u", u=2))
+
+        def quant(i, d):
+            codes = work.tile([P, B], U32, name="hidq", bufs=6, align_bytes=64)
+            scales = work.tile([P, B], U8, name="hids", bufs=6, align_bytes=64)
+            hid[i, d] = (codes, scales)
+            nc.vector.quantize_mx(out=codes[:].bitcast(E4M3X4), scales=scales[:], in_=grouped[i, d][:])
+
+        def second(j, c):
+            bank = psum.tile([P, H], F32, name="acc2", bufs=2)
+            acc2[j, c] = bank
+            parts = ([hid[j - 1, LR]] if j > 0 else []) + ([hid[j, RL]] if j < S - 1 else [])
+            for n, (codes, scales) in enumerate(parts):
+                nc.tensor.matmul_mx(
+                    out=bank[:],
+                    lhsT=codes[:, P * c : P * (c + 1)].bitcast(E4M3X4),
+                    lhsT_scale=scales[:, P * c : P * (c + 1)],
+                    rhs=w2[:].bitcast(E2M1X4),
+                    rhs_scale=w2s[:],
+                    start=(n == 0),
+                    stop=(n == len(parts) - 1),
+                )
+
+        def emit(j, c):
+            res = work.tile([P, H], F32, name="res", bufs=8, align_bytes=64)
+            bias = b2_twice if 0 < j < S - 1 else b2_once
+            nc.vector.tensor_tensor(out=res[:], in0=acc2[j, c][:], in1=bias[:], op=ALU.add)
+            nc.sync.dma_start(out=out[P * c : P * (c + 1), j, :], in_=res[:])
+
+        for g in range(2):
+            nc.vector.tensor_copy(out=w1[:, g, :].rearrange("p (t m b) -> p m t b", t=NT, b=2), in_=w1_raw[:, g, :].rearrange("p (m t b) -> p m t b", t=NT, b=2))
+        nc.vector.tensor_copy(out=w1s[:].rearrange("p g (t m) -> p g m t", t=NT), in_=w1s_raw[:].rearrange("p g (m t) -> p g m t", t=NT))
+        for half in range(2):
+            for j in range(2):
+                widen(j, 2 * half)
+                widen(j, 2 * half + 1)
+                turn(j, half)
+                words_out(j, half)
+                quant_h_half(j, half)
+            for d in (RL, LR):
+                for u in range(2):
+                    first_half(0, d, u, half)
+        widen(2, 0)
+        widen(2, 1)
+        nc.gpsimd.tensor_scalar(out=b2_twice[:], in0=b2_once[:], scalar1=2.0, scalar2=0.0, op0=ALU.mult, op1=ALU.add)
+
+        plan = {}
+        for i in range(S - 1):
+            for q in range(4):
+                plan[i, q] = [(i - 1, q)] if i > 0 else []
+        last = S - 2
+        plan[last, 0] = [(last - 1, 0), (last - 1, 1)]
+        plan[last, 1] = [(last - 1, 2), (last - 1, 3)]
+        plan[last, 2] = []
+        plan[last, 3] = [(last, 0), (last, 1)]
+
+        for i in range(S - 1):
+            for q in range(4):
+                d = RL if q < 2 else LR
+                for t in (2 * (q % 2), 2 * (q % 2) + 1):
+                    if i == 0 or (i == last and d == LR):
+                        continue
+                    first(i, d, t)
+                    relu(i, d, t)
+                if i == last and d == LR:
+                    for u in range(2):
+                        first_half(i, d, u, q % 2)
+                if i > 0 and q == 0:
+                    inter(i - 1, LR)
+                if i > 0 and q == 1:
+                    quant(i - 1, LR)
+                if q == 2:
+                    inter(i, RL)
+                if q == 3:
+                    quant(i, RL)
+                if q < 2 and i + 2 < S:
+                    widen(i + 2, 2 + q)
+                if q >= 2 and i + 3 < S:
+                    widen(i + 3, q - 2)
+                for j, c in plan[i, q]:
+                    second(j, c)
+                    emit(j, c)
+                if q == 1 and i + 2 < S:
+                    for half in range(2):
+                        turn(i + 2, half)
+                        words_out(i + 2, half)
+                if q == 3 and i + 2 < S:
+                    quant_h(i + 2)
+        for half in range(2):
+            inter_half(last, LR, half)
+            second(last, 2 + half)
+            emit(last, 2 + half)
+            quant_half(last, LR, half)
+            for c in (2 * half, 2 * half + 1):
+                second(S - 1, c)
+                emit(S - 1, c)

@@ -22,6 +22,7 @@ HALF = B // 2
 FLOPS = 2 * 2 * B * (S - 1) * (2 * H * F + F * H)
 
 RL, LR = "rl", "lr"
+PAIRED = {(1, "rl"), (2, "rl"), (3, "rl"), (4, "lr"), (5, "lr"), (6, "lr")}
 
 
 def tile_graphnetlayer_pa_t_w4_kernel(tc, h_bytes, h_scale, ew1_words, ew1_scales, eb1, ew2_words, ew2_scales, eb2, out):
@@ -66,6 +67,7 @@ def tile_graphnetlayer_pa_t_w4_kernel(tc, h_bytes, h_scale, ew1_words, ew1_scale
         nc.sync.dma_start(out=hb[:, :, 5:8, :], in_=src[:, :, 5:8, :])
         nc.sync.dma_start(out=b2_once[:], in_=eb2.partition_broadcast(P))
 
+        ctx.enter_context(tc.manual_schedule())
         x = {}
         xt = {}
         hq = {}
@@ -77,7 +79,7 @@ def tile_graphnetlayer_pa_t_w4_kernel(tc, h_bytes, h_scale, ew1_words, ew1_scale
 
         def widen(j, c):
             if j not in x:
-                x[j] = work.tile([P, NC, H], BF16, name="x", bufs=3, align_bytes=64)
+                x[j] = work.tile([P, NC, H], BF16, name="x", bufs=4, align_bytes=64)
             nc.vector.tensor_tensor(out=x[j][:, c, :], in0=hb[:, c, j, :].bitcast(FP8), in1=sc[:], op=ALU.mult)
 
         def turn(j, half):
@@ -90,7 +92,7 @@ def tile_graphnetlayer_pa_t_w4_kernel(tc, h_bytes, h_scale, ew1_words, ew1_scale
 
         def words_out(j, half):
             if j not in grouped:
-                grouped[j] = work.tile([P, NC, P, 4], BF16, name="grouped", bufs=2, align_bytes=64)
+                grouped[j] = work.tile([P, NC, P, 4], BF16, name="grouped", bufs=3, align_bytes=64)
             dst = grouped[j][:, 2 * half : 2 * half + 2, :, :].rearrange("p c r t -> p (c r t)").bitcast(F32)
             nc.scalar.copy(out=dst.rearrange("p (c r u) -> p c r u", c=2, u=2), in_=xt[j, half][:].rearrange("p c u r -> p c r u"))
 
@@ -101,7 +103,7 @@ def tile_graphnetlayer_pa_t_w4_kernel(tc, h_bytes, h_scale, ew1_words, ew1_scale
             nc.vector.quantize_mx(out=codes[:].bitcast(E4M3X4), scales=scales[:], in_=grouped[j][:].rearrange("p c r t -> p (c r t)"))
 
         def first(i, d, t):
-            bank = psum.tile([P, B], F32, name="acc1", bufs=4)
+            bank = psum.tile([P, B], F32, name="acc1", bufs=3)
             acc1[i, d, t] = bank
             nodes = (i, i + 1) if d == LR else (i + 1, i)
             for g in range(2):
@@ -116,10 +118,15 @@ def tile_graphnetlayer_pa_t_w4_kernel(tc, h_bytes, h_scale, ew1_words, ew1_scale
                     stop=(g == 1),
                 )
 
+        def plane(i, d, t):
+            if (i, d) in PAIRED:
+                return pairs[i, d][:].rearrange("p (u n e) -> p u n e", u=2, e=2)[:, t // 2, :, t % 2]
+            return pairs[i, d][:, B * t : B * (t + 1)]
+
         def relu(i, d, t):
             if (i, d) not in pairs:
-                pairs[i, d] = work.tile([P, 2, B, 2], BF16, name="pairs", bufs=3, align_bytes=64)
-            nc.scalar.activation(out=pairs[i, d][:, t // 2, :, t % 2], in_=acc1[i, d, t][:], func=ACT.Relu, bias=b1[:, t : t + 1])
+                pairs[i, d] = work.tile([P, 4 * B], BF16, name="pairs", bufs=4, align_bytes=64)
+            nc.scalar.activation(out=plane(i, d, t), in_=acc1[i, d, t][:], func=ACT.Relu, bias=b1[:, t : t + 1])
 
         def quant_h_half(j, half):
             if j not in hq:
@@ -131,7 +138,7 @@ def tile_graphnetlayer_pa_t_w4_kernel(tc, h_bytes, h_scale, ew1_words, ew1_scale
             nc.vector.quantize_mx(out=codes[:, cols].bitcast(E4M3X4), scales=scales[:, cols], in_=grouped[j][:, 2 * half : 2 * half + 2, :, :].rearrange("p c r t -> p (c r t)"))
 
         def first_half(i, d, u, half):
-            bank = psum.tile([P, 2, HALF], F32, name="acc1", bufs=4)
+            bank = psum.tile([P, 2, HALF], F32, name="acc1", bufs=3)
             nodes = (i, i + 1) if d == LR else (i + 1, i)
             for e in range(2):
                 t = 2 * u + e
@@ -148,20 +155,30 @@ def tile_graphnetlayer_pa_t_w4_kernel(tc, h_bytes, h_scale, ew1_words, ew1_scale
                             start=(g == 0),
                             stop=(g == 1),
                         )
+            acc1[i, d, u, half] = bank
+
+        def relu_half(i, d, u, half):
+            bank = acc1[i, d, u, half]
             if (i, d) not in pairs:
-                pairs[i, d] = work.tile([P, 2, B, 2], BF16, name="pairs", bufs=3, align_bytes=64)
+                pairs[i, d] = work.tile([P, 4 * B], BF16, name="pairs", bufs=4, align_bytes=64)
             for e in range(2):
                 t = 2 * u + e
-                nc.scalar.activation(out=pairs[i, d][:, u, HALF * half : HALF * (half + 1), e], in_=bank[:, e, :], func=ACT.Relu, bias=b1[:, t : t + 1])
+                nc.scalar.activation(out=plane(i, d, t)[:, HALF * half : HALF * (half + 1)], in_=bank[:, e, :], func=ACT.Relu, bias=b1[:, t : t + 1])
+
+        def inter_cols(i, d, lo, hi):
+            if (i, d) not in grouped:
+                full = work.tile([P, 4 * B], BF16, name="full", bufs=3, align_bytes=64)
+                grouped[i, d] = full
+            dst = grouped[i, d][:, 4 * lo : 4 * hi]
+            if (i, d) in PAIRED:
+                words = pairs[i, d][:].bitcast(F32).rearrange("p (u n) -> p n u", u=2)
+                nc.vector.tensor_copy(out=dst.bitcast(F32).rearrange("p (n u) -> p n u", u=2), in_=words[:, lo:hi, :])
+            else:
+                planes = pairs[i, d][:].rearrange("p (t n) -> p t n", t=NT)[:, :, lo:hi]
+                nc.vector.tensor_copy(out=dst.rearrange("p (c k t) -> p c t k", k=4, t=NT), in_=planes.rearrange("p t (c k) -> p c t k", k=4))
 
         def inter_half(i, d, half):
-            if (i, d) not in grouped:
-                full = work.tile([P, 4 * B], BF16, name="full", bufs=2, align_bytes=64)
-                grouped[i, d] = full
-            full = grouped[i, d]
-            words = pairs[i, d][:].rearrange("p u n e -> p (u n e)").bitcast(F32).rearrange("p (u n) -> p n u", u=2)
-            cols = slice(HALF * half, HALF * (half + 1))
-            nc.vector.tensor_copy(out=full[:].bitcast(F32).rearrange("p (n u) -> p n u", u=2)[:, cols, :], in_=words[:, cols, :])
+            inter_cols(i, d, HALF * half, HALF * (half + 1))
 
         def quant_half(i, d, half):
             if (i, d) not in hid:
@@ -173,10 +190,7 @@ def tile_graphnetlayer_pa_t_w4_kernel(tc, h_bytes, h_scale, ew1_words, ew1_scale
             nc.vector.quantize_mx(out=codes[:, cols].bitcast(E4M3X4), scales=scales[:, cols], in_=grouped[i, d][:, 4 * HALF * half : 4 * HALF * (half + 1)])
 
         def inter(i, d):
-            full = work.tile([P, 4 * B], BF16, name="full", bufs=2, align_bytes=64)
-            grouped[i, d] = full
-            words = pairs[i, d][:].rearrange("p u n e -> p (u n e)").bitcast(F32)
-            nc.vector.tensor_copy(out=full[:].bitcast(F32).rearrange("p (n u) -> p n u", u=2), in_=words.rearrange("p (u n) -> p n u", u=2))
+            inter_cols(i, d, 0, B)
 
         def quant(i, d):
             codes = work.tile([P, B], U32, name="hidq", bufs=6, align_bytes=64)
@@ -185,7 +199,7 @@ def tile_graphnetlayer_pa_t_w4_kernel(tc, h_bytes, h_scale, ew1_words, ew1_scale
             nc.vector.quantize_mx(out=codes[:].bitcast(E4M3X4), scales=scales[:], in_=grouped[i, d][:])
 
         def second(j, c):
-            bank = psum.tile([P, H], F32, name="acc2", bufs=2)
+            bank = psum.tile([P, H], F32, name="acc2", bufs=3)
             acc2[j, c] = bank
             parts = ([hid[j - 1, LR]] if j > 0 else []) + ([hid[j, RL]] if j < S - 1 else [])
             for n, (codes, scales) in enumerate(parts):
@@ -205,70 +219,57 @@ def tile_graphnetlayer_pa_t_w4_kernel(tc, h_bytes, h_scale, ew1_words, ew1_scale
             nc.vector.tensor_tensor(out=res[:], in0=acc2[j, c][:], in1=bias[:], op=ALU.add)
             nc.sync.dma_start(out=out[P * c : P * (c + 1), j, :], in_=res[:])
 
-        for g in range(2):
-            nc.vector.tensor_copy(out=w1[:, g, :].rearrange("p (t m b) -> p m t b", t=NT, b=2), in_=w1_raw[:, g, :].rearrange("p (m t b) -> p m t b", t=NT, b=2))
-        nc.vector.tensor_copy(out=w1s[:].rearrange("p g (t m) -> p g m t", t=NT), in_=w1s_raw[:].rearrange("p g (m t) -> p g m t", t=NT))
-        for half in range(2):
-            for j in range(2):
-                widen(j, 2 * half)
-                widen(j, 2 * half + 1)
-                turn(j, half)
-                words_out(j, half)
-                quant_h_half(j, half)
-            for d in (RL, LR):
-                for u in range(2):
-                    first_half(0, d, u, half)
-        widen(2, 0)
-        widen(2, 1)
+        nc.vector.tensor_copy(out=w1[:, 0, :].rearrange("p (t m b) -> p m t b", t=NT, b=2), in_=w1_raw[:, 0, :].rearrange("p (m t b) -> p m t b", t=NT, b=2))
+        nc.vector.tensor_copy(out=w1[:, 1, :].rearrange("p (t m b) -> p m t b", t=NT, b=2), in_=w1_raw[:, 1, :].rearrange("p (m t b) -> p m t b", t=NT, b=2))
         nc.gpsimd.tensor_scalar(out=b2_twice[:], in0=b2_once[:], scalar1=2.0, scalar2=0.0, op0=ALU.mult, op1=ALU.add)
 
-        plan = {}
-        for i in range(S - 1):
-            for q in range(4):
-                plan[i, q] = [(i - 1, q)] if i > 0 else []
-        last = S - 2
-        plan[last, 0] = [(last - 1, 0), (last - 1, 1)]
-        plan[last, 1] = [(last - 1, 2), (last - 1, 3)]
-        plan[last, 2] = []
-        plan[last, 3] = [(last, 0), (last, 1)]
+        def permute_scales():
+            nc.vector.tensor_copy(out=w1s[:].rearrange("p g (t m) -> p g m t", t=NT), in_=w1s_raw[:].rearrange("p g (m t) -> p g m t", t=NT))
 
+        events = []
+
+        def at(time, rank, fn, *args):
+            events.append((time, rank, len(events), fn, args))
+
+        at(-50 + 4.5, 0.0, permute_scales)
         for i in range(S - 1):
-            for q in range(4):
-                d = RL if q < 2 else LR
-                for t in (2 * (q % 2), 2 * (q % 2) + 1):
-                    if i == 0 or (i == last and d == LR):
-                        continue
-                    first(i, d, t)
-                    relu(i, d, t)
-                if i == last and d == LR:
-                    for u in range(2):
-                        first_half(i, d, u, q % 2)
-                if i > 0 and q == 0:
-                    inter(i - 1, LR)
-                if i > 0 and q == 1:
-                    quant(i - 1, LR)
-                if q == 2:
-                    inter(i, RL)
-                if q == 3:
-                    quant(i, RL)
-                if q < 2 and i + 2 < S:
-                    widen(i + 2, 2 + q)
-                if q >= 2 and i + 3 < S:
-                    widen(i + 3, q - 2)
-                for j, c in plan[i, q]:
-                    second(j, c)
-                    emit(j, c)
-                if q == 1 and i + 2 < S:
+            for h, d in enumerate((RL, LR)):
+                base = 8 * i + 4 * h
+                if i == 0 or (i == S - 2 and h == 1):
                     for half in range(2):
-                        turn(i + 2, half)
-                        words_out(i + 2, half)
-                if q == 3 and i + 2 < S:
-                    quant_h(i + 2)
-        for half in range(2):
-            inter_half(last, LR, half)
-            second(last, 2 + half)
-            emit(last, 2 + half)
-            quant_half(last, LR, half)
-            for c in (2 * half, 2 * half + 1):
-                second(S - 1, c)
-                emit(S - 1, c)
+                        for u in range(2):
+                            time = -50 + 12 * half + 18 + 2 * h + u if i == 0 else base + 2 * half + u
+                            at(time, 0.525, first_half, i, d, u, half)
+                            at(time, 0.917, relu_half, i, d, u, half)
+                        if i > 0:
+                            at(time + 2, 0.798, inter_half, i, d, half)
+                            at(time + 3, 0.946, quant_half, i, d, half)
+                    if i > 0:
+                        continue
+                else:
+                    for t in range(NT):
+                        at(base + t, 0.554, first, i, d, t)
+                        at(base + t, 0.864, relu, i, d, t)
+                at(base + 5, 0.445, inter, i, d)
+                at(base + 8, 0.899, quant, i, d)
+        for j in range(S):
+            for c in range(NC):
+                if j < S - 2:
+                    time = 8 * j + 2 * c + 12
+                elif j == S - 2:
+                    time = 8 * j + 2 * c + 9
+                else:
+                    time = 8 * j + 2 * c + 8
+                at(time, 0.280, second, j, c)
+                at(time + 1, 0.522, emit, j, c)
+                at(8 * j + 2 * c - 25 if j > 1 else -50 + 12 * (c // 2) + 3 * j + c % 2, 0.395, widen, j, c)
+            for half in range(2):
+                time = 8 * j + 0 * half - 16 if j > 1 else -50 + 12 * half + 3 * j + 2
+                at(time, 0.190, turn, j, half)
+                at(time + 0 if j > 1 else time, 0.510, words_out, j, half)
+                if j < 2:
+                    at(time + 11, 0.406, quant_h_half, j, half)
+            if j > 1:
+                at(8 * j - 11, 0.460, quant_h, j)
+        for event in sorted(events, key=lambda e: e[:3]):
+            event[3](*event[4])

@@ -22,7 +22,7 @@ HALF = B // 2
 FLOPS = 2 * 2 * B * (S - 1) * (2 * H * F + F * H)
 
 RL, LR = "rl", "lr"
-PAIRED = {(1, "rl"), (2, "rl"), (3, "rl"), (4, "lr"), (5, "lr"), (6, "lr")}
+PAIRED = {(0, "lr"), (1, "rl"), (2, "lr"), (2, "rl"), (3, "rl"), (4, "lr"), (4, "rl"), (5, "lr"), (6, "lr"), (6, "rl")}
 
 
 def tile_graphnetlayer_pa_t_w4_kernel(tc, h_bytes, h_scale, ew1_words, ew1_scales, eb1, ew2_words, ew2_scales, eb2, out):
@@ -34,6 +34,7 @@ def tile_graphnetlayer_pa_t_w4_kernel(tc, h_bytes, h_scale, ew1_words, ew1_scale
 
         hb = keep.tile([P, NC, S, H], U8, name="hb", align_bytes=64)
         sc = keep.tile([P, H], F32, name="sc", align_bytes=64)
+        sc4 = keep.tile([P, 4], F32, name="sc4", align_bytes=64)
         w1_raw = keep.tile([P, 2, 2 * F], U8, name="w1_raw", align_bytes=64)
         w1 = keep.tile([P, 2, 2 * F], U8, name="w1", align_bytes=64)
         w1s_raw = keep.tile([P, 2, F], U8, name="w1s_raw", align_bytes=64)
@@ -48,18 +49,19 @@ def tile_graphnetlayer_pa_t_w4_kernel(tc, h_bytes, h_scale, ew1_words, ew1_scale
 
 
         src = h_bytes.rearrange("(c p) s h -> p c s h", p=P)
-        nc.scalar.dma_start(out=sc[:], in_=h_scale.rearrange("a b k -> (a b k)").partition_broadcast(P))
-        nc.sync.dma_start(out=w1_raw[:], in_=ew1_words.rearrange("g p n -> p g n"))
+        nc.scalar.dma_start(out=sc4[:], in_=h_scale.rearrange("a b (p t) -> p (a b t)", t=4))
+        nc.scalar.dma_start(out=b1[:], in_=eb1.rearrange("(p t) -> p t", t=NT))
         nc.sync.dma_start(out=hb[:, 0:2, 0:2, :], in_=src[:, 0:2, 0:2, :])
+        nc.sync.dma_start(out=w1_raw[:], in_=ew1_words.rearrange("g p n -> p g n"))
         nc.sync.dma_start(out=hb[:, 2:4, 0:2, :], in_=src[:, 2:4, 0:2, :])
         nc.vector.memset(w1s_raw[:].rearrange("p g n -> p (g n)").bitcast(I32), 0)
         nc.vector.memset(w2s[:].bitcast(I32), 0)
         nc.vector.memset(dummy[:], 0.0)
         for q in range(4):
             nc.sync.dma_start(out=w1s_raw[32 * q : 32 * q + 4, :, :].bitcast(I32), in_=ew1_scales.bitcast(I32)[:, 4 * q : 4 * q + 4, :].rearrange("g q n -> q g n"))
-        nc.scalar.dma_start(out=b1[:], in_=eb1.rearrange("(p t) -> p t", t=NT))
         make_identity(nc, ident[:])
         nc.scalar.activation(out=dummy[:], in_=dummy[:], func=ACT.Relu)
+        nc.sync.dma_start(out=sc[:], in_=h_scale.rearrange("a b k -> (a b k)").partition_broadcast(P))
         nc.sync.dma_start(out=hb[:, :, 2:5, :], in_=src[:, :, 2:5, :])
         nc.sync.dma_start(out=w2[:], in_=ew2_words[0])
         for q in range(4):
@@ -81,6 +83,18 @@ def tile_graphnetlayer_pa_t_w4_kernel(tc, h_bytes, h_scale, ew1_words, ew1_scale
             if j not in x:
                 x[j] = work.tile([P, NC, H], BF16, name="x", bufs=4, align_bytes=64)
             nc.vector.tensor_tensor(out=x[j][:, c, :], in0=hb[:, c, j, :].bitcast(FP8), in1=sc[:], op=ALU.mult)
+
+        def cast(j, c, engine_copy):
+            if j not in x:
+                x[j] = work.tile([P, NC, H], BF16, name="x", bufs=4, align_bytes=64)
+            engine_copy(out=x[j][:, c, :], in_=hb[:, c, j, :].bitcast(FP8))
+
+        def scale_out(j, c):
+            if j not in grouped:
+                grouped[j] = work.tile([P, NC, P, 4], BF16, name="grouped", bufs=3, align_bytes=64)
+            values = xt[j, c // 2][:, c % 2, :, :].rearrange("p u r -> p (u r)").bitcast(BF16).rearrange("p (u r e) -> p r u e", u=2, e=2)
+            factors = sc4[:].rearrange("p (u e) -> p u e", u=2).unsqueeze(1).to_broadcast([P, P, 2, 2])
+            nc.vector.tensor_tensor(out=grouped[j][:, c, :, :].rearrange("p r (u e) -> p r u e", u=2), in0=values, in1=factors, op=ALU.mult)
 
         def turn(j, half):
             bank = psum.tile([P, 2, 2, P], F32, name="xt", bufs=2)
@@ -219,19 +233,22 @@ def tile_graphnetlayer_pa_t_w4_kernel(tc, h_bytes, h_scale, ew1_words, ew1_scale
             nc.vector.tensor_tensor(out=res[:], in0=acc2[j, c][:], in1=bias[:], op=ALU.add)
             nc.sync.dma_start(out=out[P * c : P * (c + 1), j, :], in_=res[:])
 
-        nc.vector.tensor_copy(out=w1[:, 0, :].rearrange("p (t m b) -> p m t b", t=NT, b=2), in_=w1_raw[:, 0, :].rearrange("p (m t b) -> p m t b", t=NT, b=2))
-        nc.vector.tensor_copy(out=w1[:, 1, :].rearrange("p (t m b) -> p m t b", t=NT, b=2), in_=w1_raw[:, 1, :].rearrange("p (m t b) -> p m t b", t=NT, b=2))
         nc.gpsimd.tensor_scalar(out=b2_twice[:], in0=b2_once[:], scalar1=2.0, scalar2=0.0, op0=ALU.mult, op1=ALU.add)
 
+        def permute_words(g):
+            nc.vector.tensor_copy(out=w1[:, g, :].rearrange("p (t m b) -> p t m b", t=NT, b=2), in_=w1_raw[:, g, :].rearrange("p (m t b) -> p t m b", t=NT, b=2))
+
         def permute_scales():
-            nc.vector.tensor_copy(out=w1s[:].rearrange("p g (t m) -> p g m t", t=NT), in_=w1s_raw[:].rearrange("p g (m t) -> p g m t", t=NT))
+            nc.vector.tensor_copy(out=w1s[:].rearrange("p g (t m) -> p g t m", t=NT), in_=w1s_raw[:].rearrange("p g (m t) -> p g t m", t=NT))
 
         events = []
 
         def at(time, rank, fn, *args):
             events.append((time, rank, len(events), fn, args))
 
-        at(-50 + 4.5, 0.0, permute_scales)
+        for g in range(2):
+            at(-50 + 4, 0.924, permute_words, g)
+        at(-50 + 12, 0.237, permute_scales)
         for i in range(S - 1):
             for h, d in enumerate((RL, LR)):
                 base = 8 * i + 4 * h
@@ -239,37 +256,43 @@ def tile_graphnetlayer_pa_t_w4_kernel(tc, h_bytes, h_scale, ew1_words, ew1_scale
                     for half in range(2):
                         for u in range(2):
                             time = -50 + 12 * half + 18 + 2 * h + u if i == 0 else base + 2 * half + u
-                            at(time, 0.525, first_half, i, d, u, half)
-                            at(time, 0.917, relu_half, i, d, u, half)
+                            at(time, 0.187, first_half, i, d, u, half)
+                            at(time, 0.545, relu_half, i, d, u, half)
                         if i > 0:
-                            at(time + 2, 0.798, inter_half, i, d, half)
-                            at(time + 3, 0.946, quant_half, i, d, half)
+                            at(time + 2, 0.317, inter_half, i, d, half)
+                            at(time + 2, 0.680, quant_half, i, d, half)
                     if i > 0:
                         continue
                 else:
                     for t in range(NT):
-                        at(base + t, 0.554, first, i, d, t)
-                        at(base + t, 0.864, relu, i, d, t)
-                at(base + 5, 0.445, inter, i, d)
-                at(base + 8, 0.899, quant, i, d)
+                        at(base + t, 0.047, first, i, d, t)
+                        at(base + t, 0.845, relu, i, d, t)
+                at(base + 4, 0.728, inter, i, d)
+                at(base + 5, 0.740, quant, i, d)
         for j in range(S):
             for c in range(NC):
                 if j < S - 2:
-                    time = 8 * j + 2 * c + 12
-                elif j == S - 2:
                     time = 8 * j + 2 * c + 9
+                elif j == S - 2:
+                    time = 8 * j + 1 * c + 7
                 else:
-                    time = 8 * j + 2 * c + 8
-                at(time, 0.280, second, j, c)
-                at(time + 1, 0.522, emit, j, c)
-                at(8 * j + 2 * c - 25 if j > 1 else -50 + 12 * (c // 2) + 3 * j + c % 2, 0.395, widen, j, c)
+                    time = 8 * j + 2 * c + 9
+                at(time, 0.842, second, j, c)
+                at(time + 1, 0.679, emit, j, c)
+                if j > 1:
+                    at(8 * j + 2 * c - 25, 0.444, widen, j, c)
+                else:
+                    time = -50 + 12 * (c // 2) + 3 * j
+                    at(time + 0.1 * (c % 2), 0.651, cast, j, c, nc.scalar.copy)
+                    at(time + 7 + 0.1 * (c % 2), 0.216, scale_out, j, c)
             for half in range(2):
-                time = 8 * j + 0 * half - 16 if j > 1 else -50 + 12 * half + 3 * j + 2
-                at(time, 0.190, turn, j, half)
-                at(time + 0 if j > 1 else time, 0.510, words_out, j, half)
-                if j < 2:
-                    at(time + 11, 0.406, quant_h_half, j, half)
+                time = 8 * j + 0 * half - 17 if j > 1 else -50 + 12 * half + 3 * j + 2
+                at(time, 0.935, turn, j, half)
+                if j > 1:
+                    at(time + 1, 0.276, words_out, j, half)
+                else:
+                    at(time + 10, 0.759, quant_h_half, j, half)
             if j > 1:
-                at(8 * j - 11, 0.460, quant_h, j)
+                at(8 * j - 11, 0.496, quant_h, j)
         for event in sorted(events, key=lambda e: e[:3]):
             event[3](*event[4])

@@ -22,7 +22,8 @@ HALF = B // 2
 FLOPS = 2 * 2 * B * (S - 1) * (2 * H * F + F * H)
 
 RL, LR = "rl", "lr"
-PAIRED = {(0, "lr"), (1, "rl"), (2, "lr"), (2, "rl"), (3, "rl"), (4, "lr"), (4, "rl"), (5, "lr"), (6, "lr"), (6, "rl")}
+PAIRED = {(2, LR), (2, RL), (3, LR), (3, RL), (4, LR), (5, LR), (5, RL), (6, LR), (6, RL)}
+SHARED_OUT = {(6, 1), (6, 3), (7, 1)}
 
 
 def tile_graphnetlayer_pa_t_w4_kernel(tc, h_bytes, h_scale, ew1_words, ew1_scales, eb1, ew2_words, ew2_scales, eb2, out):
@@ -44,21 +45,23 @@ def tile_graphnetlayer_pa_t_w4_kernel(tc, h_bytes, h_scale, ew1_words, ew1_scale
         b1 = keep.tile([P, NT], BF16, name="b1", align_bytes=64)
         b2_once = keep.tile([P, H], BF16, name="b2_once", align_bytes=64)
         b2_twice = keep.tile([P, H], BF16, name="b2_twice", align_bytes=64)
+        zeros = keep.tile([P, B], BF16, name="zeros", align_bytes=64)
         ident = keep.tile([P, P], F32, name="ident", align_bytes=64)
         dummy = keep.tile([P, 1], F32, name="dummy", align_bytes=64)
-
 
         src = h_bytes.rearrange("(c p) s h -> p c s h", p=P)
         nc.scalar.dma_start(out=sc4[:], in_=h_scale.rearrange("a b (p t) -> p (a b t)", t=4))
         nc.scalar.dma_start(out=b1[:], in_=eb1.rearrange("(p t) -> p t", t=NT))
-        nc.sync.dma_start(out=hb[:, 0:2, 0:2, :], in_=src[:, 0:2, 0:2, :])
+        nc.sync.dma_start(out=hb[:, 0:2, 0:1, :], in_=src[:, 0:2, 0:1, :])
         nc.sync.dma_start(out=w1_raw[:], in_=ew1_words.rearrange("g p n -> p g n"))
+        nc.sync.dma_start(out=hb[:, 0:2, 1:2, :], in_=src[:, 0:2, 1:2, :])
         nc.sync.dma_start(out=hb[:, 2:4, 0:2, :], in_=src[:, 2:4, 0:2, :])
         nc.vector.memset(w1s_raw[:].rearrange("p g n -> p (g n)").bitcast(I32), 0)
         nc.vector.memset(w2s[:].bitcast(I32), 0)
         nc.vector.memset(dummy[:], 0.0)
         for q in range(4):
             nc.sync.dma_start(out=w1s_raw[32 * q : 32 * q + 4, :, :].bitcast(I32), in_=ew1_scales.bitcast(I32)[:, 4 * q : 4 * q + 4, :].rearrange("g q n -> q g n"))
+        nc.gpsimd.memset(zeros[:], 0.0)
         make_identity(nc, ident[:])
         nc.scalar.activation(out=dummy[:], in_=dummy[:], func=ACT.Relu)
         nc.sync.dma_start(out=sc[:], in_=h_scale.rearrange("a b k -> (a b k)").partition_broadcast(P))
@@ -71,152 +74,148 @@ def tile_graphnetlayer_pa_t_w4_kernel(tc, h_bytes, h_scale, ew1_words, ew1_scale
 
         ctx.enter_context(tc.manual_schedule())
         x = {}
-        xt = {}
-        hq = {}
-        pairs = {}
+        turned = {}
         grouped = {}
-        hid = {}
+        node = {}
         acc1 = {}
+        planes = {}
+        full = {}
+        hid = {}
         acc2 = {}
+        sums = {}
 
-        def widen(j, c):
+        def warm(count):
+            bank = psum.tile([P, B], F32, name="acc2", bufs=3)
+            for n in range(count):
+                nc.tensor.matmul(out=bank[:], lhsT=zeros[:, :P], rhs=zeros[:], start=True, stop=True)
+
+        def permute_words(g):
+            nc.vector.tensor_copy(out=w1[:, g, :].rearrange("p (t m b) -> p t m b", t=NT, b=2), in_=w1_raw[:, g, :].rearrange("p (m t b) -> p t m b", t=NT, b=2))
+
+        def permute_scales():
+            nc.vector.tensor_copy(out=w1s[:].rearrange("p g (t m) -> p g t m", t=NT), in_=w1s_raw[:].rearrange("p g (m t) -> p g t m", t=NT))
+
+        def node_rows(j):
             if j not in x:
-                x[j] = work.tile([P, NC, H], BF16, name="x", bufs=4, align_bytes=64)
-            nc.vector.tensor_tensor(out=x[j][:, c, :], in0=hb[:, c, j, :].bitcast(FP8), in1=sc[:], op=ALU.mult)
+                x[j] = work.tile([P, NC, H], BF16, name="x", bufs=5, align_bytes=64)
+            return x[j]
 
-        def cast(j, c, engine_copy):
-            if j not in x:
-                x[j] = work.tile([P, NC, H], BF16, name="x", bufs=4, align_bytes=64)
-            engine_copy(out=x[j][:, c, :], in_=hb[:, c, j, :].bitcast(FP8))
-
-        def scale_out(j, c):
+        def node_groups(j):
             if j not in grouped:
                 grouped[j] = work.tile([P, NC, P, 4], BF16, name="grouped", bufs=3, align_bytes=64)
-            values = xt[j, c // 2][:, c % 2, :, :].rearrange("p u r -> p (u r)").bitcast(BF16).rearrange("p (u r e) -> p r u e", u=2, e=2)
-            factors = sc4[:].rearrange("p (u e) -> p u e", u=2).unsqueeze(1).to_broadcast([P, P, 2, 2])
-            nc.vector.tensor_tensor(out=grouped[j][:, c, :, :].rearrange("p r (u e) -> p r u e", u=2), in0=values, in1=factors, op=ALU.mult)
+            return grouped[j]
+
+        def widen_only(j, c):
+            nc.scalar.copy(out=node_rows(j)[:, c, :], in_=hb[:, c, j, :].bitcast(FP8))
+
+        def widen_and_scale(j, c):
+            nc.vector.tensor_tensor(out=node_rows(j)[:, c, :], in0=hb[:, c, j, :].bitcast(FP8), in1=sc[:], op=ALU.mult)
 
         def turn(j, half):
-            bank = psum.tile([P, 2, 2, P], F32, name="xt", bufs=2)
-            xt[j, half] = bank
-            for cc in range(2):
-                words = x[j][:, 2 * half + cc, :].bitcast(F32)
+            bank = psum.tile([P, 2, 2, P], F32, name="turned", bufs=2)
+            turned[j, half] = bank
+            for c in range(2):
+                words = x[j][:, 2 * half + c, :].bitcast(F32)
                 for u in range(2):
-                    nc.tensor.transpose(bank[:, cc, u, :], words[:, u : 2 * P : 2], ident[:])
+                    nc.tensor.transpose(bank[:, c, u, :], words[:, u : 2 * P : 2], ident[:])
 
-        def words_out(j, half):
-            if j not in grouped:
-                grouped[j] = work.tile([P, NC, P, 4], BF16, name="grouped", bufs=3, align_bytes=64)
-            dst = grouped[j][:, 2 * half : 2 * half + 2, :, :].rearrange("p c r t -> p (c r t)").bitcast(F32)
-            nc.scalar.copy(out=dst.rearrange("p (c r u) -> p c r u", c=2, u=2), in_=xt[j, half][:].rearrange("p c u r -> p c r u"))
+        def scale_turned(j, c):
+            values = turned[j, c // 2][:, c % 2, :, :].rearrange("p u r -> p (u r)").bitcast(BF16)
+            factors = sc4[:].rearrange("p (u e) -> p u e", u=2).unsqueeze(1).to_broadcast([P, P, 2, 2])
+            nc.vector.tensor_tensor(
+                out=node_groups(j)[:, c, :, :].rearrange("p r (u e) -> p r u e", u=2),
+                in0=values.rearrange("p (u r e) -> p r u e", u=2, e=2),
+                in1=factors,
+                op=ALU.mult,
+            )
 
-        def quant_h(j):
-            codes = keep.tile([P, B], U32, name="hq%d" % j, align_bytes=64)
-            scales = keep.tile([P, B], U8, name="hs%d" % j, align_bytes=64)
-            hq[j] = (codes, scales)
-            nc.vector.quantize_mx(out=codes[:].bitcast(E4M3X4), scales=scales[:], in_=grouped[j][:].rearrange("p c r t -> p (c r t)"))
+        def copy_turned(j, half):
+            dst = node_groups(j)[:, 2 * half : 2 * half + 2, :, :].rearrange("p c r t -> p (c r t)").bitcast(F32)
+            nc.scalar.copy(out=dst.rearrange("p (c r u) -> p c r u", c=2, u=2), in_=turned[j, half][:].rearrange("p c u r -> p c r u"))
 
-        def first(i, d, t):
-            bank = psum.tile([P, B], F32, name="acc1", bufs=3)
-            acc1[i, d, t] = bank
+        def quantize_chains(j, lo, hi):
+            if j not in node:
+                codes = keep.tile([P, B], U32, name="codes%d" % j, align_bytes=64)
+                scales = keep.tile([P, B], U8, name="scales%d" % j, align_bytes=64)
+                node[j] = (codes, scales)
+            codes, scales = node[j]
+            values = grouped[j][:].rearrange("p c r t -> p (c r t)")[:, 4 * lo : 4 * hi]
+            nc.vector.quantize_mx(out=codes[:, lo:hi].bitcast(E4M3X4), scales=scales[:, lo:hi], in_=values)
+
+        def quantize_nodes(j):
+            quantize_chains(j, 0, B)
+
+        def quantize_nodes_half(j, half):
+            quantize_chains(j, HALF * half, HALF * (half + 1))
+
+        def edge_pass(bank_cols, i, d, t, cols):
             nodes = (i, i + 1) if d == LR else (i + 1, i)
             for g in range(2):
-                codes, scales = hq[nodes[g]]
+                codes, scales = node[nodes[g]]
                 nc.tensor.matmul_mx(
-                    out=bank[:],
-                    lhsT=w1[:, g, 256 * t : 256 * (t + 1)].bitcast(E2M1X4),
+                    out=bank_cols,
+                    lhsT=w1[:, g, 2 * P * t : 2 * P * (t + 1)].bitcast(E2M1X4),
                     lhsT_scale=w1s[:, g, P * t : P * (t + 1)],
-                    rhs=codes[:].bitcast(E4M3X4),
-                    rhs_scale=scales[:],
+                    rhs=codes[:, cols].bitcast(E4M3X4),
+                    rhs_scale=scales[:, cols],
                     start=(g == 0),
                     stop=(g == 1),
                 )
 
-        def plane(i, d, t):
-            if (i, d) in PAIRED:
-                return pairs[i, d][:].rearrange("p (u n e) -> p u n e", u=2, e=2)[:, t // 2, :, t % 2]
-            return pairs[i, d][:, B * t : B * (t + 1)]
+        def first_matmuls(i, d, t):
+            bank = psum.tile([P, B], F32, name="acc1", bufs=3)
+            acc1[i, d, t] = bank
+            edge_pass(bank[:], i, d, t, slice(0, B))
 
-        def relu(i, d, t):
-            if (i, d) not in pairs:
-                pairs[i, d] = work.tile([P, 4 * B], BF16, name="pairs", bufs=4, align_bytes=64)
+        def first_matmuls_half(i, d, u, half):
+            if d == LR and 1:
+                bank = psum.tile([P, 2, HALF], F32, name="acc2", bufs=3)
+            else:
+                bank = psum.tile([P, 2, HALF], F32, name="acc1", bufs=3)
+            acc1[i, d, u, half] = bank
+            for e in range(2):
+                for c in range(2):
+                    lo = HALF * half + P * c
+                    edge_pass(bank[:, e, P * c : P * (c + 1)], i, d, 2 * u + e, slice(lo, lo + P))
+
+        def plane(i, d, t):
+            if (i, d) not in planes:
+                planes[i, d] = work.tile([P, NT * B], BF16, name="planes", bufs=4, align_bytes=64)
+            if (i, d) in PAIRED:
+                return planes[i, d][:].rearrange("p (u n e) -> p u n e", u=2, e=2)[:, t // 2, :, t % 2]
+            return planes[i, d][:, B * t : B * (t + 1)]
+
+        def relu_out(i, d, t):
             nc.scalar.activation(out=plane(i, d, t), in_=acc1[i, d, t][:], func=ACT.Relu, bias=b1[:, t : t + 1])
 
-        def quant_h_half(j, half):
-            if j not in hq:
-                codes = keep.tile([P, B], U32, name="hq%d" % j, align_bytes=64)
-                scales = keep.tile([P, B], U8, name="hs%d" % j, align_bytes=64)
-                hq[j] = (codes, scales)
-            codes, scales = hq[j]
-            cols = slice(HALF * half, HALF * (half + 1))
-            nc.vector.quantize_mx(out=codes[:, cols].bitcast(E4M3X4), scales=scales[:, cols], in_=grouped[j][:, 2 * half : 2 * half + 2, :, :].rearrange("p c r t -> p (c r t)"))
-
-        def first_half(i, d, u, half):
-            bank = psum.tile([P, 2, HALF], F32, name="acc1", bufs=3)
-            nodes = (i, i + 1) if d == LR else (i + 1, i)
+        def relu_out_half(i, d, u, half):
             for e in range(2):
                 t = 2 * u + e
-                for c in range(2):
-                    cols = slice(HALF * half + P * c, HALF * half + P * (c + 1))
-                    for g in range(2):
-                        codes, scales = hq[nodes[g]]
-                        nc.tensor.matmul_mx(
-                            out=bank[:, e, P * c : P * (c + 1)],
-                            lhsT=w1[:, g, 256 * t : 256 * (t + 1)].bitcast(E2M1X4),
-                            lhsT_scale=w1s[:, g, P * t : P * (t + 1)],
-                            rhs=codes[:, cols].bitcast(E4M3X4),
-                            rhs_scale=scales[:, cols],
-                            start=(g == 0),
-                            stop=(g == 1),
-                        )
-            acc1[i, d, u, half] = bank
+                nc.scalar.activation(out=plane(i, d, t)[:, HALF * half : HALF * (half + 1)], in_=acc1[i, d, u, half][:, e, :], func=ACT.Relu, bias=b1[:, t : t + 1])
 
-        def relu_half(i, d, u, half):
-            bank = acc1[i, d, u, half]
-            if (i, d) not in pairs:
-                pairs[i, d] = work.tile([P, 4 * B], BF16, name="pairs", bufs=4, align_bytes=64)
-            for e in range(2):
-                t = 2 * u + e
-                nc.scalar.activation(out=plane(i, d, t)[:, HALF * half : HALF * (half + 1)], in_=bank[:, e, :], func=ACT.Relu, bias=b1[:, t : t + 1])
-
-        def inter_cols(i, d, lo, hi):
-            if (i, d) not in grouped:
-                full = work.tile([P, 4 * B], BF16, name="full", bufs=3, align_bytes=64)
-                grouped[i, d] = full
-            dst = grouped[i, d][:, 4 * lo : 4 * hi]
+        def interleave(i, d):
+            dst = work.tile([P, NT * B], BF16, name="full", bufs=3, align_bytes=64)
+            full[i, d] = dst
             if (i, d) in PAIRED:
-                words = pairs[i, d][:].bitcast(F32).rearrange("p (u n) -> p n u", u=2)
-                nc.vector.tensor_copy(out=dst.bitcast(F32).rearrange("p (n u) -> p n u", u=2), in_=words[:, lo:hi, :])
+                words = planes[i, d][:].bitcast(F32).rearrange("p (u n) -> p n u", u=2)
+                nc.vector.tensor_copy(out=dst[:].bitcast(F32).rearrange("p (n u) -> p n u", u=2), in_=words)
             else:
-                planes = pairs[i, d][:].rearrange("p (t n) -> p t n", t=NT)[:, :, lo:hi]
-                nc.vector.tensor_copy(out=dst.rearrange("p (c k t) -> p c t k", k=4, t=NT), in_=planes.rearrange("p t (c k) -> p c t k", k=4))
+                nc.vector.tensor_copy(
+                    out=dst[:].rearrange("p (c k t) -> p c t k", k=4, t=NT),
+                    in_=planes[i, d][:].rearrange("p (t c k) -> p c t k", k=4, t=NT),
+                )
 
-        def inter_half(i, d, half):
-            inter_cols(i, d, HALF * half, HALF * (half + 1))
-
-        def quant_half(i, d, half):
-            if (i, d) not in hid:
-                codes = work.tile([P, B], U32, name="hidq", bufs=6, align_bytes=64)
-                scales = work.tile([P, B], U8, name="hids", bufs=6, align_bytes=64)
-                hid[i, d] = (codes, scales)
-            codes, scales = hid[i, d]
-            cols = slice(HALF * half, HALF * (half + 1))
-            nc.vector.quantize_mx(out=codes[:, cols].bitcast(E4M3X4), scales=scales[:, cols], in_=grouped[i, d][:, 4 * HALF * half : 4 * HALF * (half + 1)])
-
-        def inter(i, d):
-            inter_cols(i, d, 0, B)
-
-        def quant(i, d):
-            codes = work.tile([P, B], U32, name="hidq", bufs=6, align_bytes=64)
-            scales = work.tile([P, B], U8, name="hids", bufs=6, align_bytes=64)
+        def quantize_hidden(i, d):
+            codes = work.tile([P, B], U32, name="hid_codes", bufs=8, align_bytes=64)
+            scales = work.tile([P, B], U8, name="hid_scales", bufs=8, align_bytes=64)
             hid[i, d] = (codes, scales)
-            nc.vector.quantize_mx(out=codes[:].bitcast(E4M3X4), scales=scales[:], in_=grouped[i, d][:])
+            nc.vector.quantize_mx(out=codes[:].bitcast(E4M3X4), scales=scales[:], in_=full[i, d][:])
 
-        def second(j, c):
+        def second_matmuls(j, c):
             bank = psum.tile([P, H], F32, name="acc2", bufs=3)
             acc2[j, c] = bank
-            parts = ([hid[j - 1, LR]] if j > 0 else []) + ([hid[j, RL]] if j < S - 1 else [])
-            for n, (codes, scales) in enumerate(parts):
+            messages = ([hid[j - 1, LR]] if j > 0 else []) + ([hid[j, RL]] if j < S - 1 else [])
+            for n, (codes, scales) in enumerate(messages):
                 nc.tensor.matmul_mx(
                     out=bank[:],
                     lhsT=codes[:, P * c : P * (c + 1)].bitcast(E4M3X4),
@@ -224,7 +223,7 @@ def tile_graphnetlayer_pa_t_w4_kernel(tc, h_bytes, h_scale, ew1_words, ew1_scale
                     rhs=w2[:].bitcast(E2M1X4),
                     rhs_scale=w2s[:],
                     start=(n == 0),
-                    stop=(n == len(parts) - 1),
+                    stop=(n == len(messages) - 1),
                 )
 
         def emit(j, c):
@@ -233,66 +232,72 @@ def tile_graphnetlayer_pa_t_w4_kernel(tc, h_bytes, h_scale, ew1_words, ew1_scale
             nc.vector.tensor_tensor(out=res[:], in0=acc2[j, c][:], in1=bias[:], op=ALU.add)
             nc.sync.dma_start(out=out[P * c : P * (c + 1), j, :], in_=res[:])
 
+        def copy_sums(j, c):
+            sums[j, c] = work.tile([P, H], F32, name="sums", bufs=3, align_bytes=64)
+            nc.scalar.copy(out=sums[j, c][:], in_=acc2[j, c][:])
+
+        def emit_on_gpsimd(j, c):
+            res = work.tile([P, H], F32, name="res_gpsimd", bufs=3, align_bytes=64)
+            bias = b2_twice if 0 < j < S - 1 else b2_once
+            nc.gpsimd.tensor_tensor(out=res[:], in0=sums[j, c][:], in1=bias[:], op=ALU.add)
+            nc.sync.dma_start(out=out[P * c : P * (c + 1), j, :], in_=res[:])
+
         nc.gpsimd.tensor_scalar(out=b2_twice[:], in0=b2_once[:], scalar1=2.0, scalar2=0.0, op0=ALU.mult, op1=ALU.add)
 
-        def permute_words(g):
-            nc.vector.tensor_copy(out=w1[:, g, :].rearrange("p (t m b) -> p t m b", t=NT, b=2), in_=w1_raw[:, g, :].rearrange("p (m t b) -> p t m b", t=NT, b=2))
+        order = [warm, quantize_nodes, quantize_hidden, first_matmuls, permute_scales, turn, first_matmuls_half, emit, widen_and_scale, copy_sums, scale_turned, widen_only, copy_turned, permute_words, interleave, second_matmuls, relu_out, relu_out_half, quantize_nodes_half, emit_on_gpsimd]
+        steps = []
 
-        def permute_scales():
-            nc.vector.tensor_copy(out=w1s[:].rearrange("p g (t m) -> p g t m", t=NT), in_=w1s_raw[:].rearrange("p g (m t) -> p g t m", t=NT))
-
-        events = []
-
-        def at(time, rank, fn, *args):
-            events.append((time, rank, len(events), fn, args))
+        def at(slot, action, *args):
+            steps.append((slot, order.index(action), action, args))
 
         for g in range(2):
-            at(-50 + 4, 0.924, permute_words, g)
-        at(-50 + 12, 0.237, permute_scales)
-        for i in range(S - 1):
-            for h, d in enumerate((RL, LR)):
+            at(-50 + 0, permute_words, g)
+        at(-50 + 8, permute_scales)
+        for j in range(2):
+            for half in range(2):
+                base = -50 + 12 * half + 3 * j
+                for c in range(2):
+                    at(base + 0.1 * c, widen_only, j, 2 * half + c)
+                    at(base + 5 + 0.1 * c, scale_turned, j, 2 * half + c)
+                at(base + 2, turn, j, half)
+                at(base + 2 + 8, quantize_nodes_half, j, half)
+        for j in range(2, S):
+            for c in range(NC):
+                at(8 * j + 2 * c - 30, widen_and_scale, j, c)
+            for half in range(2):
+                at(8 * j - 19, turn, j, half)
+                at(8 * j - 19 + 1, copy_turned, j, half)
+            at(8 * j - 13, quantize_nodes, j)
+        for h, d in enumerate((RL, LR)):
+            for half in range(2):
+                for u in range(2):
+                    at(-50 + 20 + 12 * half + 2 * h + u, first_matmuls_half, 0, d, u, half)
+                    at(-50 + 20 + 12 * half + 2 * h + u, relu_out_half, 0, d, u, half)
+            for i in range(S - 1):
                 base = 8 * i + 4 * h
-                if i == 0 or (i == S - 2 and h == 1):
-                    for half in range(2):
-                        for u in range(2):
-                            time = -50 + 12 * half + 18 + 2 * h + u if i == 0 else base + 2 * half + u
-                            at(time, 0.187, first_half, i, d, u, half)
-                            at(time, 0.545, relu_half, i, d, u, half)
-                        if i > 0:
-                            at(time + 2, 0.317, inter_half, i, d, half)
-                            at(time + 2, 0.680, quant_half, i, d, half)
-                    if i > 0:
-                        continue
-                else:
+                if i > 0:
                     for t in range(NT):
-                        at(base + t, 0.047, first, i, d, t)
-                        at(base + t, 0.845, relu, i, d, t)
-                at(base + 4, 0.728, inter, i, d)
-                at(base + 5, 0.740, quant, i, d)
+                        at(base + t, first_matmuls, i, d, t)
+                        at(base + t, relu_out, i, d, t)
+                at(base + 3 + 2, interleave, i, d)
+                at(base + 3 + 2 + 2, quantize_hidden, i, d)
         for j in range(S):
             for c in range(NC):
                 if j < S - 2:
-                    time = 8 * j + 2 * c + 9
+                    slot = 8 * j + 2 * c + 15
                 elif j == S - 2:
-                    time = 8 * j + 1 * c + 7
+                    slot = 8 * j + 1 * c + 7
                 else:
-                    time = 8 * j + 2 * c + 9
-                at(time, 0.842, second, j, c)
-                at(time + 1, 0.679, emit, j, c)
-                if j > 1:
-                    at(8 * j + 2 * c - 25, 0.444, widen, j, c)
+                    slot = 8 * j + 2 * c + 9
+                at(slot, second_matmuls, j, c)
+                if (j, c) in SHARED_OUT:
+                    at(slot + 1, copy_sums, j, c)
+                    at(slot + 5.5, emit_on_gpsimd, j, c)
                 else:
-                    time = -50 + 12 * (c // 2) + 3 * j
-                    at(time + 0.1 * (c % 2), 0.651, cast, j, c, nc.scalar.copy)
-                    at(time + 7 + 0.1 * (c % 2), 0.216, scale_out, j, c)
-            for half in range(2):
-                time = 8 * j + 0 * half - 17 if j > 1 else -50 + 12 * half + 3 * j + 2
-                at(time, 0.935, turn, j, half)
-                if j > 1:
-                    at(time + 1, 0.276, words_out, j, half)
-                else:
-                    at(time + 10, 0.759, quant_h_half, j, half)
-            if j > 1:
-                at(8 * j - 11, 0.496, quant_h, j)
-        for event in sorted(events, key=lambda e: e[:3]):
-            event[3](*event[4])
+                    at(slot + 1, emit, j, c)
+
+        at(-60, warm, 6)
+        for slot in (-47.5, -44.5, -35.5):
+            at(slot, warm, 1)
+        for slot, rank, action, args in sorted(steps, key=lambda step: step[:2]):
+            action(*args)

@@ -22,8 +22,8 @@ HALF = B // 2
 FLOPS = 2 * 2 * B * (S - 1) * (2 * H * F + F * H)
 
 RL, LR = "rl", "lr"
-PAIRED = {(2, LR), (2, RL), (3, LR), (3, RL), (4, LR), (5, LR), (5, RL), (6, LR), (6, RL)}
-SHARED_OUT = {(6, 1), (6, 3), (7, 1)}
+PAIRED = {(0, LR), (2, LR), (2, RL), (3, LR), (3, RL), (4, LR), (5, LR), (5, RL), (6, LR), (6, RL)}
+SHARED_OUT = {(6, 1), (6, 3)}
 
 
 def tile_graphnetlayer_pa_t_w4_kernel(tc, h_bytes, h_scale, ew1_words, ew1_scales, eb1, ew2_words, ew2_scales, eb2, out):
@@ -55,17 +55,18 @@ def tile_graphnetlayer_pa_t_w4_kernel(tc, h_bytes, h_scale, ew1_words, ew1_scale
         nc.sync.dma_start(out=hb[:, 0:2, 0:1, :], in_=src[:, 0:2, 0:1, :])
         nc.sync.dma_start(out=w1_raw[:], in_=ew1_words.rearrange("g p n -> p g n"))
         nc.sync.dma_start(out=hb[:, 0:2, 1:2, :], in_=src[:, 0:2, 1:2, :])
-        nc.sync.dma_start(out=hb[:, 2:4, 0:2, :], in_=src[:, 2:4, 0:2, :])
+        nc.vector.memset(zeros[:], 0.0)
         nc.vector.memset(w1s_raw[:].rearrange("p g n -> p (g n)").bitcast(I32), 0)
         nc.vector.memset(w2s[:].bitcast(I32), 0)
         nc.vector.memset(dummy[:], 0.0)
         for q in range(4):
             nc.sync.dma_start(out=w1s_raw[32 * q : 32 * q + 4, :, :].bitcast(I32), in_=ew1_scales.bitcast(I32)[:, 4 * q : 4 * q + 4, :].rearrange("g q n -> q g n"))
-        nc.gpsimd.memset(zeros[:], 0.0)
+        nc.sync.dma_start(out=hb[:, 2:4, 0:2, :], in_=src[:, 2:4, 0:2, :])
+        nc.sync.dma_start(out=hb[:, :, 2:3, :], in_=src[:, :, 2:3, :])
         make_identity(nc, ident[:])
         nc.scalar.activation(out=dummy[:], in_=dummy[:], func=ACT.Relu)
         nc.sync.dma_start(out=sc[:], in_=h_scale.rearrange("a b k -> (a b k)").partition_broadcast(P))
-        nc.sync.dma_start(out=hb[:, :, 2:5, :], in_=src[:, :, 2:5, :])
+        nc.sync.dma_start(out=hb[:, :, 3:5, :], in_=src[:, :, 3:5, :])
         nc.sync.dma_start(out=w2[:], in_=ew2_words[0])
         for q in range(4):
             nc.sync.dma_start(out=w2s[32 * q : 32 * q + 4, :].bitcast(I32), in_=ew2_scales[0].bitcast(I32)[4 * q : 4 * q + 4, :])
@@ -89,11 +90,15 @@ def tile_graphnetlayer_pa_t_w4_kernel(tc, h_bytes, h_scale, ew1_words, ew1_scale
             for n in range(count):
                 nc.tensor.matmul(out=bank[:], lhsT=zeros[:, :P], rhs=zeros[:], start=True, stop=True)
 
-        def permute_words(g):
-            nc.vector.tensor_copy(out=w1[:, g, :].rearrange("p (t m b) -> p t m b", t=NT, b=2), in_=w1_raw[:, g, :].rearrange("p (m t b) -> p t m b", t=NT, b=2))
+        def permute_words(g, u):
+            permuted = w1[:, g, :].rearrange("p (t m b) -> p t m b", t=NT, b=2)
+            arrived = w1_raw[:, g, :].rearrange("p (m t b) -> p t m b", t=NT, b=2)
+            nc.vector.tensor_copy(out=permuted[:, 2 * u : 2 * u + 2, :, :], in_=arrived[:, 2 * u : 2 * u + 2, :, :])
 
-        def permute_scales():
-            nc.vector.tensor_copy(out=w1s[:].rearrange("p g (t m) -> p g t m", t=NT), in_=w1s_raw[:].rearrange("p g (m t) -> p g t m", t=NT))
+        def permute_scales(u):
+            permuted = w1s[:].rearrange("p g (t m) -> p g t m", t=NT)
+            arrived = w1s_raw[:].rearrange("p g (m t) -> p g t m", t=NT)
+            nc.vector.tensor_copy(out=permuted[:, :, 2 * u : 2 * u + 2, :], in_=arrived[:, :, 2 * u : 2 * u + 2, :])
 
         def node_rows(j):
             if j not in x:
@@ -244,35 +249,37 @@ def tile_graphnetlayer_pa_t_w4_kernel(tc, h_bytes, h_scale, ew1_words, ew1_scale
 
         nc.gpsimd.tensor_scalar(out=b2_twice[:], in0=b2_once[:], scalar1=2.0, scalar2=0.0, op0=ALU.mult, op1=ALU.add)
 
-        order = [warm, quantize_nodes, quantize_hidden, first_matmuls, permute_scales, turn, first_matmuls_half, emit, widen_and_scale, copy_sums, scale_turned, widen_only, copy_turned, permute_words, interleave, second_matmuls, relu_out, relu_out_half, quantize_nodes_half, emit_on_gpsimd]
+        order = [warm, first_matmuls_half, permute_words, first_matmuls, quantize_hidden, emit, copy_sums, scale_turned, widen_only, quantize_nodes_half, turn, interleave, widen_and_scale, permute_scales, second_matmuls, copy_turned, quantize_nodes, relu_out, relu_out_half, emit_on_gpsimd]
         steps = []
 
         def at(slot, action, *args):
             steps.append((slot, order.index(action), action, args))
 
-        for g in range(2):
-            at(-50 + 0, permute_words, g)
-        at(-50 + 8, permute_scales)
+        for u, words_slot, scales_slot in ((0, 6, 9), (1, 7, 22)):
+            for g in range(2):
+                at(-50 + words_slot, permute_words, g, u)
+            at(-50 + scales_slot, permute_scales, u)
         for j in range(2):
             for half in range(2):
                 base = -50 + 12 * half + 3 * j
                 for c in range(2):
                     at(base + 0.1 * c, widen_only, j, 2 * half + c)
-                    at(base + 5 + 0.1 * c, scale_turned, j, 2 * half + c)
+                    at(base + 8 + 0.1 * c, scale_turned, j, 2 * half + c)
                 at(base + 2, turn, j, half)
-                at(base + 2 + 8, quantize_nodes_half, j, half)
+                at(base + 2 + 12, quantize_nodes_half, j, half)
         for j in range(2, S):
+            shift = {2: (-5, -9, -2), 3: (-3, -7, -2), 4: (2, 4, 1)}.get(j, (0, 0, 0))
             for c in range(NC):
-                at(8 * j + 2 * c - 30, widen_and_scale, j, c)
+                at(8 * j + 2 * c - 30 + shift[0], widen_and_scale, j, c)
             for half in range(2):
-                at(8 * j - 19, turn, j, half)
-                at(8 * j - 19 + 1, copy_turned, j, half)
-            at(8 * j - 13, quantize_nodes, j)
+                at(8 * j - 19 + shift[1], turn, j, half)
+                at(8 * j - 19 + 1 + shift[1], copy_turned, j, half)
+            at(8 * j - 15 + shift[2], quantize_nodes, j)
         for h, d in enumerate((RL, LR)):
             for half in range(2):
                 for u in range(2):
-                    at(-50 + 20 + 12 * half + 2 * h + u, first_matmuls_half, 0, d, u, half)
-                    at(-50 + 20 + 12 * half + 2 * h + u, relu_out_half, 0, d, u, half)
+                    at(-50 + 24 + 12 * half + 1 * h + 2 * u, first_matmuls_half, 0, d, u, half)
+                    at(-50 + 24 + 12 * half + 1 * h + 2 * u, relu_out_half, 0, d, u, half)
             for i in range(S - 1):
                 base = 8 * i + 4 * h
                 if i > 0:
@@ -284,11 +291,11 @@ def tile_graphnetlayer_pa_t_w4_kernel(tc, h_bytes, h_scale, ew1_words, ew1_scale
         for j in range(S):
             for c in range(NC):
                 if j < S - 2:
-                    slot = 8 * j + 2 * c + 15
+                    slot = 8 * j + 2 * c + 13
                 elif j == S - 2:
                     slot = 8 * j + 1 * c + 7
                 else:
-                    slot = 8 * j + 2 * c + 9
+                    slot = 8 * j + 2 * c + 5
                 at(slot, second_matmuls, j, c)
                 if (j, c) in SHARED_OUT:
                     at(slot + 1, copy_sums, j, c)

from contextlib import ExitStack

import concourse.mybir as mybir
from concourse.masks import make_identity

F32 = mybir.dt.float32
BF16 = mybir.dt.bfloat16
I32 = mybir.dt.int32
U32 = mybir.dt.uint32
U8 = mybir.dt.uint8
FP8 = mybir.dt.float8_e4m3fn
E4M3X4 = mybir.dt.float8_e4m3fn_x4
E2M1X4 = mybir.dt.float4_e2m1fn_x4
ALU = mybir.AluOpType
ACT = mybir.ActivationFunctionType

P = 128
B, S, H, F = 512, 8, 512, 512
NC = B // P
NT = F // P
HALF = B // 2
FLOPS = 2 * 2 * B * (S - 1) * (2 * H * F + F * H)

RL, LR = "rl", "lr"
PAIRED = {(0, LR), (2, LR), (2, RL), (3, LR), (3, RL), (4, LR), (5, LR), (5, RL), (6, LR), (6, RL)}
SHARED_OUT = {(6, 1), (6, 3)}


def tile_graphnetlayer_pa_t_w4_kernel(tc, h_bytes, h_scale, ew1_words, ew1_scales, eb1, ew2_words, ew2_scales, eb2, out):
    nc = tc.nc
    with ExitStack() as ctx:
        keep = ctx.enter_context(tc.tile_pool(name="keep", bufs=1))
        work = ctx.enter_context(tc.tile_pool(name="work", bufs=2))
        psum = ctx.enter_context(tc.psum_pool(name="psum", bufs=1))

        hb = keep.tile([P, NC, S, H], U8, name="hb", align_bytes=64)
        sc = keep.tile([P, H], F32, name="sc", align_bytes=64)
        sc4 = keep.tile([P, 4], F32, name="sc4", align_bytes=64)
        w1_raw = keep.tile([P, 2, 2 * F], U8, name="w1_raw", align_bytes=64)
        w1 = keep.tile([P, 2, 2 * F], U8, name="w1", align_bytes=64)
        w1s_raw = keep.tile([P, 2, F], U8, name="w1s_raw", align_bytes=64)
        w1s = keep.tile([P, 2, F], U8, name="w1s", align_bytes=64)
        w2 = keep.tile([P, 2 * H], U8, name="w2", align_bytes=64)
        w2s = keep.tile([P, H], U8, name="w2s", align_bytes=64)
        b1 = keep.tile([P, NT], BF16, name="b1", align_bytes=64)
        b2_once = keep.tile([P, H], BF16, name="b2_once", align_bytes=64)
        b2_twice = keep.tile([P, H], BF16, name="b2_twice", align_bytes=64)
        zeros = keep.tile([P, B], BF16, name="zeros", align_bytes=64)
        ident = keep.tile([P, P], F32, name="ident", align_bytes=64)
        dummy = keep.tile([P, 1], F32, name="dummy", align_bytes=64)

        src = h_bytes.rearrange("(c p) s h -> p c s h", p=P)
        nc.scalar.dma_start(out=sc4[:], in_=h_scale.rearrange("a b (p t) -> p (a b t)", t=4))
        nc.scalar.dma_start(out=b1[:], in_=eb1.rearrange("(p t) -> p t", t=NT))
        nc.sync.dma_start(out=hb[:, 0:2, 0:1, :], in_=src[:, 0:2, 0:1, :])
        nc.sync.dma_start(out=w1_raw[:], in_=ew1_words.rearrange("g p n -> p g n"))
        nc.sync.dma_start(out=hb[:, 0:2, 1:2, :], in_=src[:, 0:2, 1:2, :])
        nc.vector.memset(zeros[:], 0.0)
        nc.vector.memset(w1s_raw[:].rearrange("p g n -> p (g n)").bitcast(I32), 0)
        nc.vector.memset(w2s[:].bitcast(I32), 0)
        nc.vector.memset(dummy[:], 0.0)
        for q in range(4):
            nc.sync.dma_start(out=w1s_raw[32 * q : 32 * q + 4, :, :].bitcast(I32), in_=ew1_scales.bitcast(I32)[:, 4 * q : 4 * q + 4, :].rearrange("g q n -> q g n"))
        nc.sync.dma_start(out=hb[:, 2:4, 0:2, :], in_=src[:, 2:4, 0:2, :])
        nc.sync.dma_start(out=hb[:, :, 2:3, :], in_=src[:, :, 2:3, :])
        make_identity(nc, ident[:])
        nc.scalar.activation(out=dummy[:], in_=dummy[:], func=ACT.Relu)
        nc.sync.dma_start(out=sc[:], in_=h_scale.rearrange("a b k -> (a b k)").partition_broadcast(P))
        nc.sync.dma_start(out=hb[:, :, 3:5, :], in_=src[:, :, 3:5, :])
        nc.sync.dma_start(out=w2[:], in_=ew2_words[0])
        for q in range(4):
            nc.sync.dma_start(out=w2s[32 * q : 32 * q + 4, :].bitcast(I32), in_=ew2_scales[0].bitcast(I32)[4 * q : 4 * q + 4, :])
        nc.sync.dma_start(out=hb[:, :, 5:8, :], in_=src[:, :, 5:8, :])
        nc.sync.dma_start(out=b2_once[:], in_=eb2.partition_broadcast(P))

        ctx.enter_context(tc.manual_schedule())
        x = {}
        turned = {}
        grouped = {}
        node = {}
        acc1 = {}
        planes = {}
        full = {}
        hid = {}
        acc2 = {}
        sums = {}

        def warm(count):
            bank = psum.tile([P, B], F32, name="acc2", bufs=3)
            for n in range(count):
                nc.tensor.matmul(out=bank[:], lhsT=zeros[:, :P], rhs=zeros[:], start=True, stop=True)

        def permute_words(g, u):
            permuted = w1[:, g, :].rearrange("p (t m b) -> p t m b", t=NT, b=2)
            arrived = w1_raw[:, g, :].rearrange("p (m t b) -> p t m b", t=NT, b=2)
            nc.vector.tensor_copy(out=permuted[:, 2 * u : 2 * u + 2, :, :], in_=arrived[:, 2 * u : 2 * u + 2, :, :])

        def permute_scales(u):
            permuted = w1s[:].rearrange("p g (t m) -> p g t m", t=NT)
            arrived = w1s_raw[:].rearrange("p g (m t) -> p g t m", t=NT)
            nc.vector.tensor_copy(out=permuted[:, :, 2 * u : 2 * u + 2, :], in_=arrived[:, :, 2 * u : 2 * u + 2, :])

        def node_rows(j):
            if j not in x:
                x[j] = work.tile([P, NC, H], BF16, name="x", bufs=5, align_bytes=64)
            return x[j]

        def node_groups(j):
            if j not in grouped:
                grouped[j] = work.tile([P, NC, P, 4], BF16, name="grouped", bufs=3, align_bytes=64)
            return grouped[j]

        def widen_only(j, c):
            nc.scalar.copy(out=node_rows(j)[:, c, :], in_=hb[:, c, j, :].bitcast(FP8))

        def widen_and_scale(j, c):
            nc.vector.tensor_tensor(out=node_rows(j)[:, c, :], in0=hb[:, c, j, :].bitcast(FP8), in1=sc[:], op=ALU.mult)

        def turn(j, half):
            bank = psum.tile([P, 2, 2, P], F32, name="turned", bufs=2)
            turned[j, half] = bank
            for c in range(2):
                words = x[j][:, 2 * half + c, :].bitcast(F32)
                for u in range(2):
                    nc.tensor.transpose(bank[:, c, u, :], words[:, u : 2 * P : 2], ident[:])

        def scale_turned(j, c):
            values = turned[j, c // 2][:, c % 2, :, :].rearrange("p u r -> p (u r)").bitcast(BF16)
            factors = sc4[:].rearrange("p (u e) -> p u e", u=2).unsqueeze(1).to_broadcast([P, P, 2, 2])
            nc.vector.tensor_tensor(
                out=node_groups(j)[:, c, :, :].rearrange("p r (u e) -> p r u e", u=2),
                in0=values.rearrange("p (u r e) -> p r u e", u=2, e=2),
                in1=factors,
                op=ALU.mult,
            )

        def copy_turned(j, half):
            dst = node_groups(j)[:, 2 * half : 2 * half + 2, :, :].rearrange("p c r t -> p (c r t)").bitcast(F32)
            nc.scalar.copy(out=dst.rearrange("p (c r u) -> p c r u", c=2, u=2), in_=turned[j, half][:].rearrange("p c u r -> p c r u"))

        def quantize_chains(j, lo, hi):
            if j not in node:
                codes = keep.tile([P, B], U32, name="codes%d" % j, align_bytes=64)
                scales = keep.tile([P, B], U8, name="scales%d" % j, align_bytes=64)
                node[j] = (codes, scales)
            codes, scales = node[j]
            values = grouped[j][:].rearrange("p c r t -> p (c r t)")[:, 4 * lo : 4 * hi]
            nc.vector.quantize_mx(out=codes[:, lo:hi].bitcast(E4M3X4), scales=scales[:, lo:hi], in_=values)

        def quantize_nodes(j):
            quantize_chains(j, 0, B)

        def quantize_nodes_half(j, half):
            quantize_chains(j, HALF * half, HALF * (half + 1))

        def edge_pass(bank_cols, i, d, t, cols):
            nodes = (i, i + 1) if d == LR else (i + 1, i)
            for g in range(2):
                codes, scales = node[nodes[g]]
                nc.tensor.matmul_mx(
                    out=bank_cols,
                    lhsT=w1[:, g, 2 * P * t : 2 * P * (t + 1)].bitcast(E2M1X4),
                    lhsT_scale=w1s[:, g, P * t : P * (t + 1)],
                    rhs=codes[:, cols].bitcast(E4M3X4),
                    rhs_scale=scales[:, cols],
                    start=(g == 0),
                    stop=(g == 1),
                )

        def first_matmuls(i, d, t):
            bank = psum.tile([P, B], F32, name="acc1", bufs=3)
            acc1[i, d, t] = bank
            edge_pass(bank[:], i, d, t, slice(0, B))

        def first_matmuls_half(i, d, u, half):
            if d == LR and 1:
                bank = psum.tile([P, 2, HALF], F32, name="acc2", bufs=3)
            else:
                bank = psum.tile([P, 2, HALF], F32, name="acc1", bufs=3)
            acc1[i, d, u, half] = bank
            for e in range(2):
                for c in range(2):
                    lo = HALF * half + P * c
                    edge_pass(bank[:, e, P * c : P * (c + 1)], i, d, 2 * u + e, slice(lo, lo + P))

        def plane(i, d, t):
            if (i, d) not in planes:
                planes[i, d] = work.tile([P, NT * B], BF16, name="planes", bufs=4, align_bytes=64)
            if (i, d) in PAIRED:
                return planes[i, d][:].rearrange("p (u n e) -> p u n e", u=2, e=2)[:, t // 2, :, t % 2]
            return planes[i, d][:, B * t : B * (t + 1)]

        def relu_out(i, d, t):
            nc.scalar.activation(out=plane(i, d, t), in_=acc1[i, d, t][:], func=ACT.Relu, bias=b1[:, t : t + 1])

        def relu_out_half(i, d, u, half):
            for e in range(2):
                t = 2 * u + e
                nc.scalar.activation(out=plane(i, d, t)[:, HALF * half : HALF * (half + 1)], in_=acc1[i, d, u, half][:, e, :], func=ACT.Relu, bias=b1[:, t : t + 1])

        def interleave(i, d):
            dst = work.tile([P, NT * B], BF16, name="full", bufs=3, align_bytes=64)
            full[i, d] = dst
            if (i, d) in PAIRED:
                words = planes[i, d][:].bitcast(F32).rearrange("p (u n) -> p n u", u=2)
                nc.vector.tensor_copy(out=dst[:].bitcast(F32).rearrange("p (n u) -> p n u", u=2), in_=words)
            else:
                nc.vector.tensor_copy(
                    out=dst[:].rearrange("p (c k t) -> p c t k", k=4, t=NT),
                    in_=planes[i, d][:].rearrange("p (t c k) -> p c t k", k=4, t=NT),
                )

        def quantize_hidden(i, d):
            codes = work.tile([P, B], U32, name="hid_codes", bufs=8, align_bytes=64)
            scales = work.tile([P, B], U8, name="hid_scales", bufs=8, align_bytes=64)
            hid[i, d] = (codes, scales)
            nc.vector.quantize_mx(out=codes[:].bitcast(E4M3X4), scales=scales[:], in_=full[i, d][:])

        def second_matmuls(j, c):
            bank = psum.tile([P, H], F32, name="acc2", bufs=3)
            acc2[j, c] = bank
            messages = ([hid[j - 1, LR]] if j > 0 else []) + ([hid[j, RL]] if j < S - 1 else [])
            for n, (codes, scales) in enumerate(messages):
                nc.tensor.matmul_mx(
                    out=bank[:],
                    lhsT=codes[:, P * c : P * (c + 1)].bitcast(E4M3X4),
                    lhsT_scale=scales[:, P * c : P * (c + 1)],
                    rhs=w2[:].bitcast(E2M1X4),
                    rhs_scale=w2s[:],
                    start=(n == 0),
                    stop=(n == len(messages) - 1),
                )

        def emit(j, c):
            res = work.tile([P, H], F32, name="res", bufs=8, align_bytes=64)
            bias = b2_twice if 0 < j < S - 1 else b2_once
            nc.vector.tensor_tensor(out=res[:], in0=acc2[j, c][:], in1=bias[:], op=ALU.add)
            nc.sync.dma_start(out=out[P * c : P * (c + 1), j, :], in_=res[:])

        def copy_sums(j, c):
            sums[j, c] = work.tile([P, H], F32, name="sums", bufs=3, align_bytes=64)
            nc.scalar.copy(out=sums[j, c][:], in_=acc2[j, c][:])

        def emit_on_gpsimd(j, c):
            res = work.tile([P, H], F32, name="res_gpsimd", bufs=3, align_bytes=64)
            bias = b2_twice if 0 < j < S - 1 else b2_once
            nc.gpsimd.tensor_tensor(out=res[:], in0=sums[j, c][:], in1=bias[:], op=ALU.add)
            nc.sync.dma_start(out=out[P * c : P * (c + 1), j, :], in_=res[:])

        nc.gpsimd.tensor_scalar(out=b2_twice[:], in0=b2_once[:], scalar1=2.0, scalar2=0.0, op0=ALU.mult, op1=ALU.add)

        order = [warm, first_matmuls_half, permute_words, first_matmuls, quantize_hidden, emit, copy_sums, scale_turned, widen_only, quantize_nodes_half, turn, interleave, widen_and_scale, permute_scales, second_matmuls, copy_turned, quantize_nodes, relu_out, relu_out_half, emit_on_gpsimd]
        steps = []

        def at(slot, action, *args):
            steps.append((slot, order.index(action), action, args))

        for u, words_slot, scales_slot in ((0, 6, 9), (1, 7, 22)):
            for g in range(2):
                at(-50 + words_slot, permute_words, g, u)
            at(-50 + scales_slot, permute_scales, u)
        for j in range(2):
            for half in range(2):
                base = -50 + 12 * half + 3 * j
                for c in range(2):
                    at(base + 0.1 * c, widen_only, j, 2 * half + c)
                    at(base + 8 + 0.1 * c, scale_turned, j, 2 * half + c)
                at(base + 2, turn, j, half)
                at(base + 2 + 12, quantize_nodes_half, j, half)
        for j in range(2, S):
            shift = {2: (-5, -9, -2), 3: (-3, -7, -2), 4: (2, 4, 1)}.get(j, (0, 0, 0))
            for c in range(NC):
                at(8 * j + 2 * c - 30 + shift[0], widen_and_scale, j, c)
            for half in range(2):
                at(8 * j - 19 + shift[1], turn, j, half)
                at(8 * j - 19 + 1 + shift[1], copy_turned, j, half)
            at(8 * j - 15 + shift[2], quantize_nodes, j)
        for h, d in enumerate((RL, LR)):
            for half in range(2):
                for u in range(2):
                    at(-50 + 24 + 12 * half + 1 * h + 2 * u, first_matmuls_half, 0, d, u, half)
                    at(-50 + 24 + 12 * half + 1 * h + 2 * u, relu_out_half, 0, d, u, half)
            for i in range(S - 1):
                base = 8 * i + 4 * h
                if i > 0:
                    for t in range(NT):
                        at(base + t, first_matmuls, i, d, t)
                        at(base + t, relu_out, i, d, t)
                at(base + 3 + 2, interleave, i, d)
                at(base + 3 + 2 + 2, quantize_hidden, i, d)
        for j in range(S):
            for c in range(NC):
                if j < S - 2:
                    slot = 8 * j + 2 * c + 13
                elif j == S - 2:
                    slot = 8 * j + 1 * c + 7
                else:
                    slot = 8 * j + 2 * c + 5
                at(slot, second_matmuls, j, c)
                if (j, c) in SHARED_OUT:
                    at(slot + 1, copy_sums, j, c)
                    at(slot + 5.5, emit_on_gpsimd, j, c)
                else:
                    at(slot + 1, emit, j, c)

        at(-60, warm, 6)
        for slot in (-47.5, -44.5, -35.5):
            at(slot, warm, 1)
        for slot, rank, action, args in sorted(steps, key=lambda step: step[:2]):
            action(*args)
